import numpy as np
import ml_dtypes


def mxq(x, axis, fmt="e4m3"):
    dtype, down = {"e4m3": (ml_dtypes.float8_e4m3fn, 7), "e5m2": (ml_dtypes.float8_e5m2, 14)}[fmt]
    v = np.moveaxis(np.asarray(x, np.float32).astype(ml_dtypes.bfloat16).astype(np.float64), axis, -1)
    blocks = v.reshape(v.shape[:-1] + (-1, 32))
    amax = np.abs(blocks).max(-1, keepdims=True)
    byte = np.maximum(np.where(amax > 0, np.frexp(amax)[1] - 1 + 127, 0) - down, 1)
    scale = np.exp2(byte - 127.0)
    codes = (blocks / scale).astype(np.float32).astype(dtype).astype(np.float64)
    return np.moveaxis((codes * scale).reshape(v.shape), -1, axis)


WIDE = False


def mx_kscale(k):
    if not WIDE:
        return np.ones(k)
    levels = np.array([10, -10, 5, -5, 0])
    a = np.random.permutation(np.resize(levels, k // 512 * 4)).reshape(k // 512, 4)
    idx = np.arange(k)
    return np.exp2(a[idx // 512, idx % 128 // 32])


BF16 = ml_dtypes.bfloat16


def bf(x):
    return np.asarray(x, np.float32).astype(BF16)


def f64(x):
    return np.asarray(x).astype(np.float64)


B, H = 8192, 512
DMN_FACTOR = 0.5


def sigmoid(v):
    return 1.0 / (1.0 + np.exp(-v))


def setup_inputs():
    s = mx_kscale(H)
    return {"x": bf(np.random.standard_normal((B, H)) * s),
            "W": bf(np.random.standard_normal((H, H)) / np.sqrt(H) / s[None, :]),
            "b": bf(np.random.standard_normal(H) * 0.1),
            "plasticity_modulation": bf(np.random.uniform(0.0, 1.0, H) / s),
            "connectivity_mask": bf(np.random.uniform(0.0, 1.0, (H, H)) * 6.0 * np.sqrt(H))}


def reference(x, W, b, plasticity_modulation, connectivity_mask):
    x = f64(x)
    hn = x.shape[1]
    bdnf_effect = sigmoid((mxq(x, 1, "e4m3") @ mxq(f64(W), 1, "e4m3").T) + f64(b))
    xs = x * f64(plasticity_modulation)
    g = mxq(xs, 1, "e4m3") @ mxq(f64(connectivity_mask), 1, "e4m3").T
    fi = xs * g * (DMN_FACTOR / hn)
    return xs + bdnf_effect * fi

@@ -1,0 +1,284 @@
+from contextlib import ExitStack
+
+import concourse.mybir as mybir
+from concourse.masks import make_identity
+
+F32 = mybir.dt.float32
+BF16 = mybir.dt.bfloat16
+U32 = mybir.dt.uint32
+U8 = mybir.dt.uint8
+FP8X4 = mybir.dt.float8_e4m3fn_x4
+ALU = mybir.AluOpType
+ACT = mybir.ActivationFunctionType
+
+P = 128
+B = 8192
+H = 512
+ROWS = 512
+NM = B // ROWS
+NJ = H // P
+UNITS = NM * NJ
+SCALE = 0.5 / H
+
+FLOPS = 2 * 2 * B * H * H
+
+
+def tile_neuroplasticitymodule_t_kernel(
+    tc, x, W, b, plasticity_modulation, connectivity_mask, out
+):
+    nc = tc.nc
+    with ExitStack() as ctx:
+        ctx.enter_context(tc.manual_schedule())
+        const = ctx.enter_context(tc.tile_pool(name="const", bufs=1))
+        grp = ctx.enter_context(tc.tile_pool(name="grp", bufs=2))
+        cod = ctx.enter_context(tc.tile_pool(name="cod", bufs=2))
+        ew = ctx.enter_context(tc.tile_pool(name="ew", bufs=3))
+        outp = ctx.enter_context(tc.tile_pool(name="outp", bufs=3))
+        ps = ctx.enter_context(tc.psum_pool(name="ps", bufs=2))
+
+        vt = const.tile([P, 384], BF16, name="vt")
+        nc.vector.memset(vt[:], 0.0)
+        warm = const.tile([P, 2], F32, name="warm")
+        nc.vector.memset(warm[:], 0.0)
+        nc.scalar.activation(out=warm[:, 1:2], in_=warm[:, 0:1], func=ACT.Sigmoid)
+        ident_f = const.tile([P, P], F32, name="ident_f")
+        make_identity(nc, ident_f[:])
+        ident_b = const.tile([P, P], BF16, name="ident_b")
+        make_identity(nc, ident_b[:])
+
+        w_nat = const.tile([P, NJ, H], BF16, name="w_nat")
+        c_nat = const.tile([P, NJ, H], BF16, name="c_nat")
+        x_nat = [const.tile([P, 4, H], BF16, name="x_nat%d" % m) for m in range(NM)]
+        x_view = x.rearrange("(m r i) k -> m r (i k)", r=P, i=4)
+        out_view = out.rearrange("(m r i) j -> m r i j", r=P, i=4)
+
+        nc.sync.dma_start(out=x_nat[0][:].rearrange("p i k -> p (i k)"), in_=x_view[0])
+        nc.sync.dma_start(
+            out=vt[0:2, 128:384], in_=plasticity_modulation.rearrange("(u w) -> u w", u=2)
+        )
+        nc.sync.dma_start(
+            out=vt[0:4, 0:128], in_=plasticity_modulation.rearrange("(a m) -> a m", a=4)
+        )
+        nc.sync.dma_start(out=vt[4:8, 0:128], in_=b.rearrange("(a m) -> a m", a=4))
+        nc.sync.dma_start(out=w_nat[:], in_=W.rearrange("(a p) k -> p a k", p=P))
+        nc.sync.dma_start(
+            out=c_nat[:], in_=connectivity_mask.rearrange("(a p) k -> p a k", p=P)
+        )
+        for m in range(1, NM):
+            nc.sync.dma_start(out=x_nat[m][:].rearrange("p i k -> p (i k)"), in_=x_view[m])
+
+        def transpose_words(src, h, tag):
+            bank = ps.tile([P, 2, 256], F32, tag=tag, name="bank_" + tag)
+            for rr in range(2):
+                words = src[:, 2 * h + rr, :].bitcast(F32)
+                for u in range(2):
+                    nc.tensor.transpose(
+                        bank[:, u, rr * P : (rr + 1) * P],
+                        words[:, u * P : (u + 1) * P],
+                        ident_f[:],
+                    )
+            return bank
+
+        def evacuate(bank, grouped, h):
+            dst = grouped[:].bitcast(F32).rearrange("p (c u) -> p c u", u=2)
+            nc.scalar.copy(
+                out=dst[:, h * 256 : (h + 1) * 256, :], in_=bank[:].rearrange("p u c -> p c u")
+            )
+
+        def quantise(grouped, codes, scales):
+            nc.vector.quantize_mx(
+                out=codes[:].bitcast(FP8X4), scales=scales[:], in_=grouped[:]
+            )
+
+        state = {}
+
+        def in_transposes(m, h):
+            state[("xb", m, h)] = transpose_words(x_nat[m], h, "xin")
+
+        def in_copy(m, h):
+            if h == 0:
+                state[("gx", m)] = grp.tile(
+                    [P, 4 * ROWS], BF16, tag="gx", name="gx", align_bytes=64
+                )
+            evacuate(state[("xb", m, h)], state[("gx", m)], h)
+
+        def scale_x(m, h):
+            if h == 0:
+                state[("gxs", m)] = grp.tile(
+                    [P, 4 * ROWS], BF16, tag="gxs", name="gxs", align_bytes=64
+                )
+            half = slice(h * 2 * ROWS, (h + 1) * 2 * ROWS)
+            nc.vector.tensor_tensor(
+                out=state[("gxs", m)][:, half].rearrange("p (a c) -> p a c", a=2),
+                in0=state[("gx", m)][:, half].rearrange("p (a c) -> p a c", a=2),
+                in1=pm4[:].unsqueeze(1).to_broadcast([P, 2, ROWS]),
+                op=ALU.mult,
+            )
+
+        def quantise_x(m):
+            xc = cod.tile([P, ROWS], U32, tag="xc", name="xc", align_bytes=64)
+            xs = cod.tile([P, ROWS], U8, tag="xs", name="xs", align_bytes=64)
+            quantise(state[("gx", m)], xc, xs)
+            state[("xcodes", m)] = (xc, xs)
+
+        def quantise_xs(m):
+            yc = cod.tile([P, ROWS], U32, tag="yc", name="yc", align_bytes=64)
+            ys = cod.tile([P, ROWS], U8, tag="ys", name="ys", align_bytes=64)
+            quantise(state[("gxs", m)], yc, ys)
+            state[("ycodes", m)] = (yc, ys)
+
+        def mx(i):
+            m, jb = divmod(i, NJ)
+            cols = slice(jb * P, (jb + 1) * P)
+            xc, xs = state[("xcodes", m)]
+            yc, ys = state[("ycodes", m)]
+            z = ps.tile([P, ROWS], F32, tag="z", name="z")
+            nc.tensor.matmul_mx(
+                out=z[:],
+                lhsT=w_codes[:, cols].bitcast(FP8X4),
+                lhsT_scale=w_scales[:, cols],
+                rhs=xc[:].bitcast(FP8X4),
+                rhs_scale=xs[:],
+                start=True,
+                stop=True,
+            )
+            g = ps.tile([P, ROWS], F32, tag="g", name="g")
+            nc.tensor.matmul_mx(
+                out=g[:],
+                lhsT=c_codes[:, cols].bitcast(FP8X4),
+                lhsT_scale=c_scales[:, cols],
+                rhs=yc[:].bitcast(FP8X4),
+                rhs_scale=ys[:],
+                start=True,
+                stop=True,
+            )
+            state[("z", i)] = z
+            state[("g", i)] = g
+
+        def sigmoid(i):
+            jb = i % NJ
+            s = ew.tile([P, ROWS], F32, tag="s", name="s")
+            nc.scalar.activation(
+                out=s[:], in_=state[("z", i)][:], func=ACT.Sigmoid,
+                bias=vec[:, 4 + jb : 5 + jb], scale=1.0,
+            )
+            state[("s", i)] = s
+
+        def gate(i):
+            jb = i % NJ
+            u = ew.tile([P, ROWS], F32, tag="u", name="u")
+            nc.vector.scalar_tensor_tensor(
+                out=u[:], in0=state[("g", i)][:], scalar=cpm[:, jb : jb + 1],
+                in1=state[("s", i)][:], op0=ALU.mult, op1=ALU.mult,
+            )
+            state[("u", i)] = u
+
+        def add_pm(i):
+            jb = i % NJ
+            q = ew.tile([P, ROWS], F32, tag="q", name="q")
+            nc.scalar.activation(
+                out=q[:], in_=state[("u", i)][:], func=ACT.Identity,
+                bias=vec[:, jb : jb + 1], scale=1.0,
+            )
+            state[("q", i)] = q
+
+        def out_transposes(i):
+            t = ps.tile([P, 4, P], F32, tag="t", name="t")
+            q = state[("q", i)]
+            for rb in range(4):
+                nc.tensor.transpose(t[:, rb, :], q[:, rb * P : (rb + 1) * P], ident_f[:])
+            state[("t", i)] = t
+
+        def finish(i):
+            m, jb = divmod(i, NJ)
+            cols = slice(jb * P, (jb + 1) * P)
+            if jb == 0:
+                state[("o", m)] = outp.tile([P, 4, H], F32, tag="o", name="o")
+            o = state[("o", m)]
+            nc.vector.tensor_tensor(
+                out=o[:, :, cols], in0=state[("t", i)][:], in1=x_nat[m][:, :, cols],
+                op=ALU.mult,
+            )
+            if m < NM - 1:
+                pieces = [(0, H)] if jb == NJ - 1 else []
+            else:
+                pieces = {1: [(0, 2 * P)], 2: [(2 * P, 3 * P)], 3: [(3 * P, H)]}.get(jb, [])
+            for lo, hi in pieces:
+                nc.sync.dma_start(out=out_view[m][:, :, lo:hi], in_=o[:, :, lo:hi])
+
+        in_transposes(0, 0)
+        in_transposes(0, 1)
+        pw = ps.tile([P, P], F32, tag="t", name="pw")
+        nc.tensor.transpose(pw[:], vt[:, 128:384].bitcast(F32), ident_f[:])
+        pv = ps.tile([P, P], BF16, tag="t", name="pv")
+        nc.tensor.transpose(pv[:], vt[:, 0:128], ident_b[:])
+        w_banks = [transpose_words(w_nat, h, "z") for h in range(2)]
+        c_banks = [transpose_words(c_nat, h, "g") for h in range(2)]
+
+        in_copy(0, 0)
+        in_copy(0, 1)
+        pm4 = const.tile([P, ROWS], BF16, name="pm4", align_bytes=64)
+        nc.scalar.copy(
+            out=pm4[:].bitcast(F32).rearrange("p (c u) -> p c u", u=2),
+            in_=pw[:, 0:2].unsqueeze(1).to_broadcast([P, P, 2]),
+        )
+        w_grp = const.tile([P, 4 * H], BF16, name="w_grp", align_bytes=64)
+        c_grp = const.tile([P, 4 * H], BF16, name="c_grp", align_bytes=64)
+        for h in range(2):
+            evacuate(w_banks[h], w_grp, h)
+        for h in range(2):
+            evacuate(c_banks[h], c_grp, h)
+
+        w_codes = const.tile([P, H], U32, name="w_codes", align_bytes=64)
+        w_scales = const.tile([P, H], U8, name="w_scales", align_bytes=64)
+        c_codes = const.tile([P, H], U32, name="c_codes", align_bytes=64)
+        c_scales = const.tile([P, H], U8, name="c_scales", align_bytes=64)
+        vec = const.tile([P, 8], F32, name="vec")
+        cpm = const.tile([P, 4], F32, name="cpm")
+        quantise_x(0)
+        scale_x(0, 0)
+        scale_x(0, 1)
+        quantise(w_grp, w_codes, w_scales)
+        nc.vector.tensor_copy(out=vec[:], in_=pv[:, 0:8])
+        nc.vector.tensor_scalar_mul(out=cpm[:], in0=vec[:, 0:4], scalar1=SCALE)
+        quantise_xs(0)
+        quantise(c_grp, c_codes, c_scales)
+
+        def unit(i):
+            return 0 <= i < UNITS
+
+        def tile_at(step, lead):
+            m, r = divmod(step + lead, NJ)
+            return m if (r == 0 and 1 <= m < NM) else None
+
+        for step in range(-6, UNITS + 4):
+            if unit(step - 1):
+                add_pm(step - 1)
+            if unit(step + 1):
+                mx(step + 1)
+            if unit(step - 2):
+                out_transposes(step - 2)
+            for h in range(2):
+                m = tile_at(step, 9 - h)
+                if m is not None:
+                    in_transposes(m, h)
+            if unit(step + 1):
+                sigmoid(step + 1)
+            for h in range(2):
+                m = tile_at(step, 9 - h)
+                if m is not None:
+                    in_copy(m, h)
+            if unit(step):
+                gate(step)
+            if unit(step - 3):
+                finish(step - 3)
+            for h in range(2):
+                m = tile_at(step, 7 - h)
+                if m is not None:
+                    scale_x(m, h)
+            m = tile_at(step, 5)
+            if m is not None:
+                quantise_x(m)
+            m = tile_at(step, 4)
+            if m is not None:
+                quantise_xs(m)

@@ -19,6 +19,7 @@ NM = B // ROWS
 NJ = H // P
 UNITS = NM * NJ
 SCALE = 0.5 / H
+ON_GPSIMD = 3
 
 FLOPS = 2 * 2 * B * H * H
 
@@ -30,11 +31,15 @@ def tile_neuroplasticitymodule_t_kernel(
     with ExitStack() as ctx:
         ctx.enter_context(tc.manual_schedule())
         const = ctx.enter_context(tc.tile_pool(name="const", bufs=1))
-        grp = ctx.enter_context(tc.tile_pool(name="grp", bufs=2))
+        grp = ctx.enter_context(tc.tile_pool(name="grp", bufs=3))
+        grs = ctx.enter_context(tc.tile_pool(name="grs", bufs=1))
         cod = ctx.enter_context(tc.tile_pool(name="cod", bufs=2))
-        ew = ctx.enter_context(tc.tile_pool(name="ew", bufs=3))
+        ew = ctx.enter_context(tc.tile_pool(name="ew", bufs=4))
         outp = ctx.enter_context(tc.tile_pool(name="outp", bufs=3))
-        ps = ctx.enter_context(tc.psum_pool(name="ps", bufs=2))
+        ps1 = ctx.enter_context(tc.psum_pool(name="ps1", bufs=1))
+        ps2 = ctx.enter_context(tc.psum_pool(name="ps2", bufs=2))
+        ps3 = ctx.enter_context(tc.psum_pool(name="ps3", bufs=3))
+        pools = {"xin": ps1, "z": ps2, "t": ps2, "g": ps3}
 
         vt = const.tile([P, 384], BF16, name="vt")
         nc.vector.memset(vt[:], 0.0)
@@ -68,7 +73,7 @@ def tile_neuroplasticitymodule_t_kernel(
             nc.sync.dma_start(out=x_nat[m][:].rearrange("p i k -> p (i k)"), in_=x_view[m])
 
         def transpose_words(src, h, tag):
-            bank = ps.tile([P, 2, 256], F32, tag=tag, name="bank_" + tag)
+            bank = pools[tag].tile([P, 2, 256], F32, tag=tag, name="bank_" + tag)
             for rr in range(2):
                 words = src[:, 2 * h + rr, :].bitcast(F32)
                 for u in range(2):
@@ -92,8 +97,8 @@ def tile_neuroplasticitymodule_t_kernel(
 
         state = {}
 
-        def in_transposes(m, h):
-            state[("xb", m, h)] = transpose_words(x_nat[m], h, "xin")
+        def in_transposes(m, h, tag="xin"):
+            state[("xb", m, h)] = transpose_words(x_nat[m], h, tag)
 
         def in_copy(m, h):
             if h == 0:
@@ -102,18 +107,19 @@ def tile_neuroplasticitymodule_t_kernel(
                 )
             evacuate(state[("xb", m, h)], state[("gx", m)], h)
 
-        def scale_x(m, h):
-            if h == 0:
-                state[("gxs", m)] = grp.tile(
-                    [P, 4 * ROWS], BF16, tag="gxs", name="gxs", align_bytes=64
+        def scale_x(m, on_gpsimd):
+            gxs = grs.tile([P, 4 * ROWS], BF16, tag="gxs", name="gxs", align_bytes=64)
+            state[("gxs", m)] = gxs
+            for k in range(on_gpsimd, 4):
+                part = slice(k * ROWS, (k + 1) * ROWS)
+                nc.vector.tensor_tensor(
+                    out=gxs[:, part], in0=state[("gx", m)][:, part], in1=pm4[:], op=ALU.mult
                 )
-            half = slice(h * 2 * ROWS, (h + 1) * 2 * ROWS)
-            nc.vector.tensor_tensor(
-                out=state[("gxs", m)][:, half].rearrange("p (a c) -> p a c", a=2),
-                in0=state[("gx", m)][:, half].rearrange("p (a c) -> p a c", a=2),
-                in1=pm4[:].unsqueeze(1).to_broadcast([P, 2, ROWS]),
-                op=ALU.mult,
-            )
+            for k in range(on_gpsimd):
+                part = slice(k * ROWS, (k + 1) * ROWS)
+                nc.gpsimd.tensor_tensor(
+                    out=gxs[:, part], in0=state[("gx", m)][:, part], in1=pm4[:], op=ALU.mult
+                )
 
         def quantise_x(m):
             xc = cod.tile([P, ROWS], U32, tag="xc", name="xc", align_bytes=64)
@@ -132,7 +138,7 @@ def tile_neuroplasticitymodule_t_kernel(
             cols = slice(jb * P, (jb + 1) * P)
             xc, xs = state[("xcodes", m)]
             yc, ys = state[("ycodes", m)]
-            z = ps.tile([P, ROWS], F32, tag="z", name="z")
+            z = ps2.tile([P, ROWS], F32, tag="z", name="z")
             nc.tensor.matmul_mx(
                 out=z[:],
                 lhsT=w_codes[:, cols].bitcast(FP8X4),
@@ -142,7 +148,7 @@ def tile_neuroplasticitymodule_t_kernel(
                 start=True,
                 stop=True,
             )
-            g = ps.tile([P, ROWS], F32, tag="g", name="g")
+            g = ps3.tile([P, ROWS], F32, tag="g", name="g")
             nc.tensor.matmul_mx(
                 out=g[:],
                 lhsT=c_codes[:, cols].bitcast(FP8X4),
@@ -183,7 +189,7 @@ def tile_neuroplasticitymodule_t_kernel(
             state[("q", i)] = q
 
         def out_transposes(i):
-            t = ps.tile([P, 4, P], F32, tag="t", name="t")
+            t = ps2.tile([P, 4, P], F32, tag="t", name="t")
             q = state[("q", i)]
             for rb in range(4):
                 nc.tensor.transpose(t[:, rb, :], q[:, rb * P : (rb + 1) * P], ident_f[:])
@@ -207,10 +213,10 @@ def tile_neuroplasticitymodule_t_kernel(
                 nc.sync.dma_start(out=out_view[m][:, :, lo:hi], in_=o[:, :, lo:hi])
 
         in_transposes(0, 0)
-        in_transposes(0, 1)
-        pw = ps.tile([P, P], F32, tag="t", name="pw")
+        in_transposes(0, 1, "g")
+        pw = ps2.tile([P, P], F32, tag="t", name="pw")
         nc.tensor.transpose(pw[:], vt[:, 128:384].bitcast(F32), ident_f[:])
-        pv = ps.tile([P, P], BF16, tag="t", name="pv")
+        pv = ps2.tile([P, P], BF16, tag="t", name="pv")
         nc.tensor.transpose(pv[:], vt[:, 0:128], ident_b[:])
         w_banks = [transpose_words(w_nat, h, "z") for h in range(2)]
         c_banks = [transpose_words(c_nat, h, "g") for h in range(2)]
@@ -237,7 +243,6 @@ def tile_neuroplasticitymodule_t_kernel(
         cpm = const.tile([P, 4], F32, name="cpm")
         quantise_x(0)
         scale_x(0, 0)
-        scale_x(0, 1)
         quantise(w_grp, w_codes, w_scales)
         nc.vector.tensor_copy(out=vec[:], in_=pv[:, 0:8])
         nc.vector.tensor_scalar_mul(out=cpm[:], in0=vec[:, 0:4], scalar1=SCALE)
@@ -251,34 +256,31 @@ def tile_neuroplasticitymodule_t_kernel(
             m, r = divmod(step + lead, NJ)
             return m if (r == 0 and 1 <= m < NM) else None
 
-        for step in range(-6, UNITS + 4):
+        for step in range(-10, UNITS + 4):
             if unit(step - 1):
                 add_pm(step - 1)
-            if unit(step + 1):
-                mx(step + 1)
+            if unit(step + 2):
+                mx(step + 2)
             if unit(step - 2):
                 out_transposes(step - 2)
             for h in range(2):
-                m = tile_at(step, 9 - h)
+                m = tile_at(step, 12 - h)
                 if m is not None:
                     in_transposes(m, h)
-            if unit(step + 1):
-                sigmoid(step + 1)
+            if unit(step + 2):
+                sigmoid(step + 2)
             for h in range(2):
-                m = tile_at(step, 9 - h)
+                m = tile_at(step, 11 - h)
                 if m is not None:
                     in_copy(m, h)
             if unit(step):
                 gate(step)
             if unit(step - 3):
                 finish(step - 3)
-            for h in range(2):
-                m = tile_at(step, 7 - h)
-                if m is not None:
-                    scale_x(m, h)
-            m = tile_at(step, 5)
+            m = tile_at(step, 3)
             if m is not None:
                 quantise_x(m)
-            m = tile_at(step, 4)
-            if m is not None:
                 quantise_xs(m)
+            m = tile_at(step, 7)
+            if m is not None:
+                scale_x(m, ON_GPSIMD)

@@ -20,6 +20,7 @@ NJ = H // P
 UNITS = NM * NJ
 SCALE = 0.5 / H
 ON_GPSIMD = 3
+LATER = {2: 6, 3: 4, 4: 3, 5: 2, 6: 1}
 
 FLOPS = 2 * 2 * B * H * H
 
@@ -31,15 +32,12 @@ def tile_neuroplasticitymodule_t_kernel(
     with ExitStack() as ctx:
         ctx.enter_context(tc.manual_schedule())
         const = ctx.enter_context(tc.tile_pool(name="const", bufs=1))
-        grp = ctx.enter_context(tc.tile_pool(name="grp", bufs=3))
-        grs = ctx.enter_context(tc.tile_pool(name="grs", bufs=1))
+        grp = ctx.enter_context(tc.tile_pool(name="grp", bufs=5))
+        grs = ctx.enter_context(tc.tile_pool(name="grs", bufs=2))
         cod = ctx.enter_context(tc.tile_pool(name="cod", bufs=2))
-        ew = ctx.enter_context(tc.tile_pool(name="ew", bufs=4))
+        ew = ctx.enter_context(tc.tile_pool(name="ew", bufs=5))
         outp = ctx.enter_context(tc.tile_pool(name="outp", bufs=3))
-        ps1 = ctx.enter_context(tc.psum_pool(name="ps1", bufs=1))
-        ps2 = ctx.enter_context(tc.psum_pool(name="ps2", bufs=2))
-        ps3 = ctx.enter_context(tc.psum_pool(name="ps3", bufs=3))
-        pools = {"xin": ps1, "z": ps2, "t": ps2, "g": ps3}
+        ps = ctx.enter_context(tc.psum_pool(name="ps", bufs=2))
 
         vt = const.tile([P, 384], BF16, name="vt")
         nc.vector.memset(vt[:], 0.0)
@@ -73,7 +71,7 @@ def tile_neuroplasticitymodule_t_kernel(
             nc.sync.dma_start(out=x_nat[m][:].rearrange("p i k -> p (i k)"), in_=x_view[m])
 
         def transpose_words(src, h, tag):
-            bank = pools[tag].tile([P, 2, 256], F32, tag=tag, name="bank_" + tag)
+            bank = ps.tile([P, 2, 256], F32, tag=tag, name="bank_" + tag)
             for rr in range(2):
                 words = src[:, 2 * h + rr, :].bitcast(F32)
                 for u in range(2):
@@ -97,8 +95,8 @@ def tile_neuroplasticitymodule_t_kernel(
 
         state = {}
 
-        def in_transposes(m, h, tag="xin"):
-            state[("xb", m, h)] = transpose_words(x_nat[m], h, tag)
+        def in_transposes(m, h):
+            state[("xb", m, h)] = transpose_words(x_nat[m], h, "xin")
 
         def in_copy(m, h):
             if h == 0:
@@ -133,12 +131,11 @@ def tile_neuroplasticitymodule_t_kernel(
             quantise(state[("gxs", m)], yc, ys)
             state[("ycodes", m)] = (yc, ys)
 
-        def mx(i):
+        def mx_z(i):
             m, jb = divmod(i, NJ)
             cols = slice(jb * P, (jb + 1) * P)
             xc, xs = state[("xcodes", m)]
-            yc, ys = state[("ycodes", m)]
-            z = ps2.tile([P, ROWS], F32, tag="z", name="z")
+            z = ps.tile([P, ROWS], F32, tag="z", name="z")
             nc.tensor.matmul_mx(
                 out=z[:],
                 lhsT=w_codes[:, cols].bitcast(FP8X4),
@@ -148,7 +145,13 @@ def tile_neuroplasticitymodule_t_kernel(
                 start=True,
                 stop=True,
             )
-            g = ps3.tile([P, ROWS], F32, tag="g", name="g")
+            state[("z", i)] = z
+
+        def mx_g(i):
+            m, jb = divmod(i, NJ)
+            cols = slice(jb * P, (jb + 1) * P)
+            yc, ys = state[("ycodes", m)]
+            g = ps.tile([P, ROWS], F32, tag="g", name="g")
             nc.tensor.matmul_mx(
                 out=g[:],
                 lhsT=c_codes[:, cols].bitcast(FP8X4),
@@ -158,7 +161,6 @@ def tile_neuroplasticitymodule_t_kernel(
                 start=True,
                 stop=True,
             )
-            state[("z", i)] = z
             state[("g", i)] = g
 
         def sigmoid(i):
@@ -189,7 +191,7 @@ def tile_neuroplasticitymodule_t_kernel(
             state[("q", i)] = q
 
         def out_transposes(i):
-            t = ps2.tile([P, 4, P], F32, tag="t", name="t")
+            t = ps.tile([P, 4, P], F32, tag="t", name="t")
             q = state[("q", i)]
             for rb in range(4):
                 nc.tensor.transpose(t[:, rb, :], q[:, rb * P : (rb + 1) * P], ident_f[:])
@@ -213,10 +215,10 @@ def tile_neuroplasticitymodule_t_kernel(
                 nc.sync.dma_start(out=out_view[m][:, :, lo:hi], in_=o[:, :, lo:hi])
 
         in_transposes(0, 0)
-        in_transposes(0, 1, "g")
-        pw = ps2.tile([P, P], F32, tag="t", name="pw")
+        in_transposes(0, 1)
+        pw = ps.tile([P, P], F32, tag="t", name="pw")
         nc.tensor.transpose(pw[:], vt[:, 128:384].bitcast(F32), ident_f[:])
-        pv = ps2.tile([P, P], BF16, tag="t", name="pv")
+        pv = ps.tile([P, P], BF16, tag="t", name="pv")
         nc.tensor.transpose(pv[:], vt[:, 0:128], ident_b[:])
         w_banks = [transpose_words(w_nat, h, "z") for h in range(2)]
         c_banks = [transpose_words(c_nat, h, "g") for h in range(2)]
@@ -252,35 +254,32 @@ def tile_neuroplasticitymodule_t_kernel(
         def unit(i):
             return 0 <= i < UNITS
 
-        def tile_at(step, lead):
-            m, r = divmod(step + lead, NJ)
-            return m if (r == 0 and 1 <= m < NM) else None
+        def prepared_at(step, lead):
+            return [m for m in range(1, NM) if NJ * m - lead + LATER.get(m, 0) == step]
 
-        for step in range(-10, UNITS + 4):
+        for step in range(-12, UNITS + 4):
             if unit(step - 1):
                 add_pm(step - 1)
             if unit(step + 2):
-                mx(step + 2)
+                mx_z(step + 2)
+            if unit(step + 1):
+                mx_g(step + 1)
             if unit(step - 2):
                 out_transposes(step - 2)
             for h in range(2):
-                m = tile_at(step, 12 - h)
-                if m is not None:
+                for m in prepared_at(step, 16 - h):
                     in_transposes(m, h)
             if unit(step + 2):
                 sigmoid(step + 2)
             for h in range(2):
-                m = tile_at(step, 11 - h)
-                if m is not None:
+                for m in prepared_at(step, 15 - h):
                     in_copy(m, h)
+            if (step + 3) % NJ == 0 and 1 <= (step + 3) // NJ < NM:
+                quantise_xs((step + 3) // NJ)
+                quantise_x((step + 3) // NJ)
+            for m in prepared_at(step, 11):
+                scale_x(m, 0 if m == 1 else ON_GPSIMD)
             if unit(step):
                 gate(step)
             if unit(step - 3):
                 finish(step - 3)
-            m = tile_at(step, 3)
-            if m is not None:
-                quantise_x(m)
-                quantise_xs(m)
-            m = tile_at(step, 7)
-            if m is not None:
-                scale_x(m, ON_GPSIMD)

@@ -19,7 +19,7 @@ NM = B // ROWS
 NJ = H // P
 UNITS = NM * NJ
 SCALE = 0.5 / H
-ON_GPSIMD = 3
+ON_GPSIMD = 1792
 LATER = {2: 6, 3: 4, 4: 3, 5: 2, 6: 1}
 
 FLOPS = 2 * 2 * B * H * H
@@ -108,16 +108,13 @@ def tile_neuroplasticitymodule_t_kernel(
         def scale_x(m, on_gpsimd):
             gxs = grs.tile([P, 4 * ROWS], BF16, tag="gxs", name="gxs", align_bytes=64)
             state[("gxs", m)] = gxs
-            for k in range(on_gpsimd, 4):
-                part = slice(k * ROWS, (k + 1) * ROWS)
-                nc.vector.tensor_tensor(
-                    out=gxs[:, part], in0=state[("gx", m)][:, part], in1=pm4[:], op=ALU.mult
-                )
-            for k in range(on_gpsimd):
-                part = slice(k * ROWS, (k + 1) * ROWS)
-                nc.gpsimd.tensor_tensor(
-                    out=gxs[:, part], in0=state[("gx", m)][:, part], in1=pm4[:], op=ALU.mult
-                )
+            for engine, first, last in ((nc.vector, on_gpsimd, 4 * ROWS), (nc.gpsimd, 0, on_gpsimd)):
+                for lo in range(first, last, ROWS):
+                    hi = min(lo + ROWS, last)
+                    engine.tensor_tensor(
+                        out=gxs[:, lo:hi], in0=state[("gx", m)][:, lo:hi], in1=pm4[:, 0 : hi - lo],
+                        op=ALU.mult,
+                    )
 
         def quantise_x(m):
             xc = cod.tile([P, ROWS], U32, tag="xc", name="xc", align_bytes=64)
@@ -279,7 +276,9 @@ def tile_neuroplasticitymodule_t_kernel(
                 quantise_x((step + 3) // NJ)
             for m in prepared_at(step, 11):
                 scale_x(m, 0 if m == 1 else ON_GPSIMD)
-            if unit(step):
+            if unit(step) and step != UNITS - 1:
                 gate(step)
+            if step == UNITS - 2:
+                gate(step + 1)
             if unit(step - 3):
                 finish(step - 3)

@@ -19,7 +19,7 @@ NM = B // ROWS
 NJ = H // P
 UNITS = NM * NJ
 SCALE = 0.5 / H
-ON_GPSIMD = 1792
+ON_GPSIMD = 3
 LATER = {2: 6, 3: 4, 4: 3, 5: 2, 6: 1}
 
 FLOPS = 2 * 2 * B * H * H
@@ -30,7 +30,6 @@ def tile_neuroplasticitymodule_t_kernel(
 ):
     nc = tc.nc
     with ExitStack() as ctx:
-        ctx.enter_context(tc.manual_schedule())
         const = ctx.enter_context(tc.tile_pool(name="const", bufs=1))
         grp = ctx.enter_context(tc.tile_pool(name="grp", bufs=5))
         grs = ctx.enter_context(tc.tile_pool(name="grs", bufs=2))
@@ -108,13 +107,16 @@ def tile_neuroplasticitymodule_t_kernel(
         def scale_x(m, on_gpsimd):
             gxs = grs.tile([P, 4 * ROWS], BF16, tag="gxs", name="gxs", align_bytes=64)
             state[("gxs", m)] = gxs
-            for engine, first, last in ((nc.vector, on_gpsimd, 4 * ROWS), (nc.gpsimd, 0, on_gpsimd)):
-                for lo in range(first, last, ROWS):
-                    hi = min(lo + ROWS, last)
-                    engine.tensor_tensor(
-                        out=gxs[:, lo:hi], in0=state[("gx", m)][:, lo:hi], in1=pm4[:, 0 : hi - lo],
-                        op=ALU.mult,
-                    )
+            for k in range(on_gpsimd, 4):
+                part = slice(k * ROWS, (k + 1) * ROWS)
+                nc.vector.tensor_tensor(
+                    out=gxs[:, part], in0=state[("gx", m)][:, part], in1=pm4[:], op=ALU.mult
+                )
+            for k in range(on_gpsimd):
+                part = slice(k * ROWS, (k + 1) * ROWS)
+                nc.gpsimd.tensor_tensor(
+                    out=gxs[:, part], in0=state[("gx", m)][:, part], in1=pm4[:], op=ALU.mult
+                )
 
         def quantise_x(m):
             xc = cod.tile([P, ROWS], U32, tag="xc", name="xc", align_bytes=64)
@@ -276,9 +278,7 @@ def tile_neuroplasticitymodule_t_kernel(
                 quantise_x((step + 3) // NJ)
             for m in prepared_at(step, 11):
                 scale_x(m, 0 if m == 1 else ON_GPSIMD)
-            if unit(step) and step != UNITS - 1:
+            if unit(step):
                 gate(step)
-            if step == UNITS - 2:
-                gate(step + 1)
             if unit(step - 3):
                 finish(step - 3)

@@ -30,6 +30,7 @@ def tile_neuroplasticitymodule_t_kernel(
 ):
     nc = tc.nc
     with ExitStack() as ctx:
+        ctx.enter_context(tc.manual_schedule())
         const = ctx.enter_context(tc.tile_pool(name="const", bufs=1))
         grp = ctx.enter_context(tc.tile_pool(name="grp", bufs=5))
         grs = ctx.enter_context(tc.tile_pool(name="grs", bufs=2))
@@ -172,11 +173,9 @@ def tile_neuroplasticitymodule_t_kernel(
             state[("s", i)] = s
 
         def gate(i):
-            jb = i % NJ
             u = ew.tile([P, ROWS], F32, tag="u", name="u")
-            nc.vector.scalar_tensor_tensor(
-                out=u[:], in0=state[("g", i)][:], scalar=cpm[:, jb : jb + 1],
-                in1=state[("s", i)][:], op0=ALU.mult, op1=ALU.mult,
+            nc.vector.tensor_tensor(
+                out=u[:], in0=state[("g", i)][:], in1=state[("s", i)][:], op=ALU.mult
             )
             state[("u", i)] = u
 
@@ -185,7 +184,7 @@ def tile_neuroplasticitymodule_t_kernel(
             q = ew.tile([P, ROWS], F32, tag="q", name="q")
             nc.scalar.activation(
                 out=q[:], in_=state[("u", i)][:], func=ACT.Identity,
-                bias=vec[:, jb : jb + 1], scale=1.0,
+                bias=vec[:, jb : jb + 1], scale=cpm[:, jb : jb + 1],
             )
             state[("q", i)] = q
 

@@ -33,7 +33,6 @@ def tile_neuroplasticitymodule_t_kernel(
         ctx.enter_context(tc.manual_schedule())
         const = ctx.enter_context(tc.tile_pool(name="const", bufs=1))
         grp = ctx.enter_context(tc.tile_pool(name="grp", bufs=5))
-        grs = ctx.enter_context(tc.tile_pool(name="grs", bufs=2))
         cod = ctx.enter_context(tc.tile_pool(name="cod", bufs=2))
         ew = ctx.enter_context(tc.tile_pool(name="ew", bufs=5))
         outp = ctx.enter_context(tc.tile_pool(name="outp", bufs=3))
@@ -83,14 +82,14 @@ def tile_neuroplasticitymodule_t_kernel(
             return bank
 
         def evacuate(bank, grouped, h):
-            dst = grouped[:].bitcast(F32).rearrange("p (c u) -> p c u", u=2)
+            dst = grouped.bitcast(F32).rearrange("p (c u) -> p c u", u=2)
             nc.scalar.copy(
                 out=dst[:, h * 256 : (h + 1) * 256, :], in_=bank[:].rearrange("p u c -> p c u")
             )
 
         def quantise(grouped, codes, scales):
             nc.vector.quantize_mx(
-                out=codes[:].bitcast(FP8X4), scales=scales[:], in_=grouped[:]
+                out=codes.bitcast(FP8X4), scales=scales, in_=grouped
             )
 
         state = {}
@@ -100,14 +99,14 @@ def tile_neuroplasticitymodule_t_kernel(
 
         def in_copy(m, h):
             if h == 0:
-                state[("gx", m)] = grp.tile(
-                    [P, 4 * ROWS], BF16, tag="gx", name="gx", align_bytes=64
-                )
+                both = grp.tile([P, 8 * ROWS], BF16, tag="gx", name="gx", align_bytes=64)
+                state[("both", m)] = both
+                state[("gx", m)] = both[:, 0 : 4 * ROWS]
+                state[("gxs", m)] = both[:, 4 * ROWS : 8 * ROWS]
             evacuate(state[("xb", m, h)], state[("gx", m)], h)
 
         def scale_x(m, on_gpsimd):
-            gxs = grs.tile([P, 4 * ROWS], BF16, tag="gxs", name="gxs", align_bytes=64)
-            state[("gxs", m)] = gxs
+            gxs = state[("gxs", m)]
             for k in range(on_gpsimd, 4):
                 part = slice(k * ROWS, (k + 1) * ROWS)
                 nc.vector.tensor_tensor(
@@ -119,17 +118,16 @@ def tile_neuroplasticitymodule_t_kernel(
                     out=gxs[:, part], in0=state[("gx", m)][:, part], in1=pm4[:], op=ALU.mult
                 )
 
-        def quantise_x(m):
-            xc = cod.tile([P, ROWS], U32, tag="xc", name="xc", align_bytes=64)
-            xs = cod.tile([P, ROWS], U8, tag="xs", name="xs", align_bytes=64)
-            quantise(state[("gx", m)], xc, xs)
-            state[("xcodes", m)] = (xc, xs)
+        def code_tiles(m):
+            codes = cod.tile([P, 2 * ROWS], U32, tag="xc", name="xc", align_bytes=64)
+            scales = cod.tile([P, 2 * ROWS], U8, tag="xs", name="xs", align_bytes=64)
+            state[("xcodes", m)] = (codes[:, 0:ROWS], scales[:, 0:ROWS])
+            state[("ycodes", m)] = (codes[:, ROWS : 2 * ROWS], scales[:, ROWS : 2 * ROWS])
+            return codes, scales
 
-        def quantise_xs(m):
-            yc = cod.tile([P, ROWS], U32, tag="yc", name="yc", align_bytes=64)
-            ys = cod.tile([P, ROWS], U8, tag="ys", name="ys", align_bytes=64)
-            quantise(state[("gxs", m)], yc, ys)
-            state[("ycodes", m)] = (yc, ys)
+        def quantise_both(m):
+            codes, scales = code_tiles(m)
+            quantise(state[("both", m)][:], codes[:], scales[:])
 
         def mx_z(i):
             m, jb = divmod(i, NJ)
@@ -140,8 +138,8 @@ def tile_neuroplasticitymodule_t_kernel(
                 out=z[:],
                 lhsT=w_codes[:, cols].bitcast(FP8X4),
                 lhsT_scale=w_scales[:, cols],
-                rhs=xc[:].bitcast(FP8X4),
-                rhs_scale=xs[:],
+                rhs=xc.bitcast(FP8X4),
+                rhs_scale=xs,
                 start=True,
                 stop=True,
             )
@@ -156,8 +154,8 @@ def tile_neuroplasticitymodule_t_kernel(
                 out=g[:],
                 lhsT=c_codes[:, cols].bitcast(FP8X4),
                 lhsT_scale=c_scales[:, cols],
-                rhs=yc[:].bitcast(FP8X4),
-                rhs_scale=ys[:],
+                rhs=yc.bitcast(FP8X4),
+                rhs_scale=ys,
                 start=True,
                 stop=True,
             )
@@ -231,9 +229,9 @@ def tile_neuroplasticitymodule_t_kernel(
         w_grp = const.tile([P, 4 * H], BF16, name="w_grp", align_bytes=64)
         c_grp = const.tile([P, 4 * H], BF16, name="c_grp", align_bytes=64)
         for h in range(2):
-            evacuate(w_banks[h], w_grp, h)
+            evacuate(w_banks[h], w_grp[:], h)
         for h in range(2):
-            evacuate(c_banks[h], c_grp, h)
+            evacuate(c_banks[h], c_grp[:], h)
 
         w_codes = const.tile([P, H], U32, name="w_codes", align_bytes=64)
         w_scales = const.tile([P, H], U8, name="w_scales", align_bytes=64)
@@ -241,13 +239,14 @@ def tile_neuroplasticitymodule_t_kernel(
         c_scales = const.tile([P, H], U8, name="c_scales", align_bytes=64)
         vec = const.tile([P, 8], F32, name="vec")
         cpm = const.tile([P, 4], F32, name="cpm")
-        quantise_x(0)
+        code_tiles(0)
+        quantise(state[("gx", 0)], *state[("xcodes", 0)])
         scale_x(0, 0)
-        quantise(w_grp, w_codes, w_scales)
+        quantise(w_grp[:], w_codes[:], w_scales[:])
         nc.vector.tensor_copy(out=vec[:], in_=pv[:, 0:8])
         nc.vector.tensor_scalar_mul(out=cpm[:], in0=vec[:, 0:4], scalar1=SCALE)
-        quantise_xs(0)
-        quantise(c_grp, c_codes, c_scales)
+        quantise(state[("gxs", 0)], *state[("ycodes", 0)])
+        quantise(c_grp[:], c_codes[:], c_scales[:])
 
         def unit(i):
             return 0 <= i < UNITS
@@ -272,11 +271,10 @@ def tile_neuroplasticitymodule_t_kernel(
             for h in range(2):
                 for m in prepared_at(step, 15 - h):
                     in_copy(m, h)
-            if (step + 3) % NJ == 0 and 1 <= (step + 3) // NJ < NM:
-                quantise_xs((step + 3) // NJ)
-                quantise_x((step + 3) // NJ)
             for m in prepared_at(step, 11):
                 scale_x(m, 0 if m == 1 else ON_GPSIMD)
+            if (step + 3) % NJ == 0 and 1 <= (step + 3) // NJ < NM:
+                quantise_both((step + 3) // NJ)
             if unit(step):
                 gate(step)
             if unit(step - 3):

@@ -19,8 +19,9 @@ NM = B // ROWS
 NJ = H // P
 UNITS = NM * NJ
 SCALE = 0.5 / H
-ON_GPSIMD = 3
-LATER = {2: 6, 3: 4, 4: 3, 5: 2, 6: 1}
+
+SHARED = (1, 3)
+GP_AFFINE = (0, 2)
 
 FLOPS = 2 * 2 * B * H * H
 
@@ -34,7 +35,7 @@ def tile_neuroplasticitymodule_t_kernel(
         const = ctx.enter_context(tc.tile_pool(name="const", bufs=1))
         grp = ctx.enter_context(tc.tile_pool(name="grp", bufs=5))
         cod = ctx.enter_context(tc.tile_pool(name="cod", bufs=2))
-        ew = ctx.enter_context(tc.tile_pool(name="ew", bufs=5))
+        ew = ctx.enter_context(tc.tile_pool(name="ew", bufs=6))
         outp = ctx.enter_context(tc.tile_pool(name="outp", bufs=3))
         ps = ctx.enter_context(tc.psum_pool(name="ps", bufs=2))
 
@@ -97,6 +98,14 @@ def tile_neuroplasticitymodule_t_kernel(
         def in_transposes(m, h):
             state[("xb", m, h)] = transpose_words(x_nat[m], h, "xin")
 
+        def shared(i):
+            m, jb = divmod(i, NJ)
+            return jb in SHARED and m < NM - 1
+
+        def gp_affine(i):
+            m, jb = divmod(i, NJ)
+            return jb in GP_AFFINE and m < NM - 1
+
         def in_copy(m, h):
             if h == 0:
                 both = grp.tile([P, 8 * ROWS], BF16, tag="gx", name="gx", align_bytes=64)
@@ -105,18 +114,15 @@ def tile_neuroplasticitymodule_t_kernel(
                 state[("gxs", m)] = both[:, 4 * ROWS : 8 * ROWS]
             evacuate(state[("xb", m, h)], state[("gx", m)], h)
 
-        def scale_x(m, on_gpsimd):
-            gxs = state[("gxs", m)]
-            for k in range(on_gpsimd, 4):
-                part = slice(k * ROWS, (k + 1) * ROWS)
-                nc.vector.tensor_tensor(
-                    out=gxs[:, part], in0=state[("gx", m)][:, part], in1=pm4[:], op=ALU.mult
-                )
-            for k in range(on_gpsimd):
-                part = slice(k * ROWS, (k + 1) * ROWS)
-                nc.gpsimd.tensor_tensor(
-                    out=gxs[:, part], in0=state[("gx", m)][:, part], in1=pm4[:], op=ALU.mult
-                )
+        def scale_x(m, h):
+            half = state[("gxs", m)][:, h * 2 * ROWS : (h + 1) * 2 * ROWS]
+            words = state[("xb", m, h)][:].rearrange("p u c -> p (u c)").bitcast(BF16)
+            nc.vector.tensor_tensor(
+                out=half.rearrange("p (c u e) -> p c u e", u=2, e=2),
+                in0=words.rearrange("p (u c e) -> p c u e", u=2, e=2),
+                in1=pm4[:].rearrange("p (c u e) -> p c u e", u=2, e=2),
+                op=ALU.mult,
+            )
 
         def code_tiles(m):
             codes = cod.tile([P, 2 * ROWS], U32, tag="xc", name="xc", align_bytes=64)
@@ -180,11 +186,17 @@ def tile_neuroplasticitymodule_t_kernel(
         def add_pm(i):
             jb = i % NJ
             q = ew.tile([P, ROWS], F32, tag="q", name="q")
+            state[("q", i)] = q
+            if gp_affine(i):
+                nc.gpsimd.tensor_scalar(
+                    out=q[:], in0=state[("u", i)][:], scalar1=cpm[:, jb : jb + 1],
+                    scalar2=vec[:, jb : jb + 1], op0=ALU.mult, op1=ALU.add,
+                )
+                return
             nc.scalar.activation(
                 out=q[:], in_=state[("u", i)][:], func=ACT.Identity,
                 bias=vec[:, jb : jb + 1], scale=cpm[:, jb : jb + 1],
             )
-            state[("q", i)] = q
 
         def out_transposes(i):
             t = ps.tile([P, 4, P], F32, tag="t", name="t")
@@ -193,16 +205,28 @@ def tile_neuroplasticitymodule_t_kernel(
                 nc.tensor.transpose(t[:, rb, :], q[:, rb * P : (rb + 1) * P], ident_f[:])
             state[("t", i)] = t
 
+        def out_copy(i):
+            if shared(i):
+                tcopy = ew.tile([P, 4, P], F32, tag="tc", name="tcopy")
+                nc.scalar.copy(out=tcopy[:], in_=state[("t", i)][:])
+                state[("tc", i)] = tcopy
+
         def finish(i):
             m, jb = divmod(i, NJ)
             cols = slice(jb * P, (jb + 1) * P)
             if jb == 0:
                 state[("o", m)] = outp.tile([P, 4, H], F32, tag="o", name="o")
             o = state[("o", m)]
-            nc.vector.tensor_tensor(
-                out=o[:, :, cols], in0=state[("t", i)][:], in1=x_nat[m][:, :, cols],
-                op=ALU.mult,
-            )
+            if shared(i):
+                nc.gpsimd.tensor_tensor(
+                    out=o[:, :, cols], in0=state[("tc", i)][:], in1=x_nat[m][:, :, cols],
+                    op=ALU.mult,
+                )
+            else:
+                nc.vector.tensor_tensor(
+                    out=o[:, :, cols], in0=state[("t", i)][:], in1=x_nat[m][:, :, cols],
+                    op=ALU.mult,
+                )
             if m < NM - 1:
                 pieces = [(0, H)] if jb == NJ - 1 else []
             else:
@@ -221,10 +245,10 @@ def tile_neuroplasticitymodule_t_kernel(
 
         in_copy(0, 0)
         in_copy(0, 1)
-        pm4 = const.tile([P, ROWS], BF16, name="pm4", align_bytes=64)
-        nc.scalar.copy(
+        pm4 = const.tile([P, 2 * ROWS], BF16, name="pm4", align_bytes=64)
+        nc.vector.tensor_copy(
             out=pm4[:].bitcast(F32).rearrange("p (c u) -> p c u", u=2),
-            in_=pw[:, 0:2].unsqueeze(1).to_broadcast([P, P, 2]),
+            in_=pw[:, 0:2].unsqueeze(1).to_broadcast([P, 2 * P, 2]),
         )
         w_grp = const.tile([P, 4 * H], BF16, name="w_grp", align_bytes=64)
         c_grp = const.tile([P, 4 * H], BF16, name="c_grp", align_bytes=64)
@@ -242,6 +266,7 @@ def tile_neuroplasticitymodule_t_kernel(
         code_tiles(0)
         quantise(state[("gx", 0)], *state[("xcodes", 0)])
         scale_x(0, 0)
+        scale_x(0, 1)
         quantise(w_grp[:], w_codes[:], w_scales[:])
         nc.vector.tensor_copy(out=vec[:], in_=pv[:, 0:8])
         nc.vector.tensor_scalar_mul(out=cpm[:], in0=vec[:, 0:4], scalar1=SCALE)
@@ -252,30 +277,33 @@ def tile_neuroplasticitymodule_t_kernel(
             return 0 <= i < UNITS
 
         def prepared_at(step, lead):
-            return [m for m in range(1, NM) if NJ * m - lead + LATER.get(m, 0) == step]
+            return [m for m in range(1, NM) if NJ * m - lead == step]
 
-        for step in range(-12, UNITS + 4):
-            if unit(step - 1):
-                add_pm(step - 1)
-            if unit(step + 2):
-                mx_z(step + 2)
+        for step in range(-7, UNITS + 4):
+            if unit(step + 3):
+                mx_z(step + 3)
             if unit(step + 1):
                 mx_g(step + 1)
-            if unit(step - 2):
-                out_transposes(step - 2)
-            for h in range(2):
-                for m in prepared_at(step, 16 - h):
+            if unit(step - 3):
+                out_transposes(step - 3)
+            for h, lead in ((0, 11), (1, 9)):
+                for m in prepared_at(step, lead):
                     in_transposes(m, h)
+            if unit(step - 2):
+                add_pm(step - 2)
             if unit(step + 2):
                 sigmoid(step + 2)
-            for h in range(2):
-                for m in prepared_at(step, 15 - h):
+            for h, lead in ((0, 10), (1, 8)):
+                for m in prepared_at(step, lead):
                     in_copy(m, h)
-            for m in prepared_at(step, 11):
-                scale_x(m, 0 if m == 1 else ON_GPSIMD)
-            if (step + 3) % NJ == 0 and 1 <= (step + 3) // NJ < NM:
-                quantise_both((step + 3) // NJ)
-            if unit(step):
-                gate(step)
-            if unit(step - 3):
-                finish(step - 3)
+            if unit(step - 4):
+                out_copy(step - 4)
+            if unit(step + 0):
+                gate(step + 0)
+            if unit(step - 4):
+                finish(step - 4)
+            for h, lead in ((0, 8), (1, 6)):
+                for m in prepared_at(step, lead):
+                    scale_x(m, h)
+            if (step + 5) % NJ == 0 and 1 <= (step + 5) // NJ < NM:
+                quantise_both((step + 5) // NJ)

@@ -21,7 +21,7 @@ UNITS = NM * NJ
 SCALE = 0.5 / H
 
 SHARED = (1, 3)
-GP_AFFINE = (0, 2)
+GP_AFFINE = (1, 3)
 
 FLOPS = 2 * 2 * B * H * H
 
@@ -52,23 +52,27 @@ def tile_neuroplasticitymodule_t_kernel(
         w_nat = const.tile([P, NJ, H], BF16, name="w_nat")
         c_nat = const.tile([P, NJ, H], BF16, name="c_nat")
         x_nat = [const.tile([P, 4, H], BF16, name="x_nat%d" % m) for m in range(NM)]
-        x_view = x.rearrange("(m r i) k -> m r (i k)", r=P, i=4)
+        x_view = x.rearrange("(m r i) k -> m r i k", r=P, i=4)
+        w_view = W.rearrange("(a p) k -> p a k", p=P)
+        c_view = connectivity_mask.rearrange("(a p) k -> p a k", p=P)
+        firsts = [slice(0, 2), slice(2, 4)]
         out_view = out.rearrange("(m r i) j -> m r i j", r=P, i=4)
 
-        nc.sync.dma_start(out=x_nat[0][:].rearrange("p i k -> p (i k)"), in_=x_view[0])
+        nc.sync.dma_start(out=x_nat[0][:, firsts[0], :], in_=x_view[0][:, firsts[0], :])
         nc.sync.dma_start(
             out=vt[0:2, 128:384], in_=plasticity_modulation.rearrange("(u w) -> u w", u=2)
         )
+        nc.sync.dma_start(out=x_nat[0][:, firsts[1], :], in_=x_view[0][:, firsts[1], :])
+        nc.sync.dma_start(out=w_nat[:, firsts[0], :], in_=w_view[:, firsts[0], :])
         nc.sync.dma_start(
             out=vt[0:4, 0:128], in_=plasticity_modulation.rearrange("(a m) -> a m", a=4)
         )
         nc.sync.dma_start(out=vt[4:8, 0:128], in_=b.rearrange("(a m) -> a m", a=4))
-        nc.sync.dma_start(out=w_nat[:], in_=W.rearrange("(a p) k -> p a k", p=P))
-        nc.sync.dma_start(
-            out=c_nat[:], in_=connectivity_mask.rearrange("(a p) k -> p a k", p=P)
-        )
+        nc.sync.dma_start(out=c_nat[:, firsts[0], :], in_=c_view[:, firsts[0], :])
+        nc.sync.dma_start(out=w_nat[:, firsts[1], :], in_=w_view[:, firsts[1], :])
+        nc.sync.dma_start(out=c_nat[:, firsts[1], :], in_=c_view[:, firsts[1], :])
         for m in range(1, NM):
-            nc.sync.dma_start(out=x_nat[m][:].rearrange("p i k -> p (i k)"), in_=x_view[m])
+            nc.sync.dma_start(out=x_nat[m][:], in_=x_view[m])
 
         def transpose_words(src, h, tag):
             bank = ps.tile([P, 2, 256], F32, tag=tag, name="bank_" + tag)
@@ -82,11 +86,9 @@ def tile_neuroplasticitymodule_t_kernel(
                     )
             return bank
 
-        def evacuate(bank, grouped, h):
+        def evacuate(copy, bank, grouped, h):
             dst = grouped.bitcast(F32).rearrange("p (c u) -> p c u", u=2)
-            nc.scalar.copy(
-                out=dst[:, h * 256 : (h + 1) * 256, :], in_=bank[:].rearrange("p u c -> p c u")
-            )
+            copy(out=dst[:, h * 256 : (h + 1) * 256, :], in_=bank[:].rearrange("p u c -> p c u"))
 
         def quantise(grouped, codes, scales):
             nc.vector.quantize_mx(
@@ -99,12 +101,10 @@ def tile_neuroplasticitymodule_t_kernel(
             state[("xb", m, h)] = transpose_words(x_nat[m], h, "xin")
 
         def shared(i):
-            m, jb = divmod(i, NJ)
-            return jb in SHARED and m < NM - 1
+            return i % NJ in SHARED and i < UNITS - NJ - 1
 
         def gp_affine(i):
-            m, jb = divmod(i, NJ)
-            return jb in GP_AFFINE and m < NM - 1
+            return i % NJ in GP_AFFINE and i < UNITS - NJ - 1
 
         def in_copy(m, h):
             if h == 0:
@@ -112,7 +112,7 @@ def tile_neuroplasticitymodule_t_kernel(
                 state[("both", m)] = both
                 state[("gx", m)] = both[:, 0 : 4 * ROWS]
                 state[("gxs", m)] = both[:, 4 * ROWS : 8 * ROWS]
-            evacuate(state[("xb", m, h)], state[("gx", m)], h)
+            evacuate(nc.scalar.copy, state[("xb", m, h)], state[("gx", m)], h)
 
         def scale_x(m, h):
             half = state[("gxs", m)][:, h * 2 * ROWS : (h + 1) * 2 * ROWS]
@@ -227,51 +227,62 @@ def tile_neuroplasticitymodule_t_kernel(
                     out=o[:, :, cols], in0=state[("t", i)][:], in1=x_nat[m][:, :, cols],
                     op=ALU.mult,
                 )
-            if m < NM - 1:
+            if m < NM - 2:
                 pieces = [(0, H)] if jb == NJ - 1 else []
+            elif jb % 2 == 1:
+                pieces = [((jb - 1) * P, (jb + 1) * P)]
             else:
-                pieces = {1: [(0, 2 * P)], 2: [(2 * P, 3 * P)], 3: [(3 * P, H)]}.get(jb, [])
+                pieces = []
             for lo, hi in pieces:
                 nc.sync.dma_start(out=out_view[m][:, :, lo:hi], in_=o[:, :, lo:hi])
 
-        in_transposes(0, 0)
-        in_transposes(0, 1)
-        pw = ps.tile([P, P], F32, tag="t", name="pw")
-        nc.tensor.transpose(pw[:], vt[:, 128:384].bitcast(F32), ident_f[:])
-        pv = ps.tile([P, P], BF16, tag="t", name="pv")
-        nc.tensor.transpose(pv[:], vt[:, 0:128], ident_b[:])
-        w_banks = [transpose_words(w_nat, h, "z") for h in range(2)]
-        c_banks = [transpose_words(c_nat, h, "g") for h in range(2)]
+        def quantise_weights(grouped, codes, scales, h):
+            cols = slice(h * 256, (h + 1) * 256)
+            quantise(grouped[:, h * 2 * H : (h + 1) * 2 * H], codes[:, cols], scales[:, cols])
 
-        in_copy(0, 0)
-        in_copy(0, 1)
-        pm4 = const.tile([P, 2 * ROWS], BF16, name="pm4", align_bytes=64)
-        nc.vector.tensor_copy(
-            out=pm4[:].bitcast(F32).rearrange("p (c u) -> p c u", u=2),
-            in_=pw[:, 0:2].unsqueeze(1).to_broadcast([P, 2 * P, 2]),
-        )
         w_grp = const.tile([P, 4 * H], BF16, name="w_grp", align_bytes=64)
         c_grp = const.tile([P, 4 * H], BF16, name="c_grp", align_bytes=64)
-        for h in range(2):
-            evacuate(w_banks[h], w_grp[:], h)
-        for h in range(2):
-            evacuate(c_banks[h], c_grp[:], h)
-
+        pm4 = const.tile([P, 2 * ROWS], BF16, name="pm4", align_bytes=64)
         w_codes = const.tile([P, H], U32, name="w_codes", align_bytes=64)
         w_scales = const.tile([P, H], U8, name="w_scales", align_bytes=64)
         c_codes = const.tile([P, H], U32, name="c_codes", align_bytes=64)
         c_scales = const.tile([P, H], U8, name="c_scales", align_bytes=64)
         vec = const.tile([P, 8], F32, name="vec")
         cpm = const.tile([P, 4], F32, name="cpm")
+
+        in_transposes(0, 0)
+        pw = ps.tile([P, P], F32, tag="t", name="pw")
+        nc.tensor.transpose(pw[:], vt[:, 128:384].bitcast(F32), ident_f[:])
+        in_transposes(0, 1)
+        w_banks = [transpose_words(w_nat, 0, "z")]
+        pv = ps.tile([P, P], BF16, tag="t", name="pv")
+        nc.tensor.transpose(pv[:], vt[:, 0:128], ident_b[:])
+        c_banks = [transpose_words(c_nat, 0, "g")]
+        w_banks.append(transpose_words(w_nat, 1, "z"))
+        c_banks.append(transpose_words(c_nat, 1, "g"))
+
+        in_copy(0, 0)
+        in_copy(0, 1)
+        evacuate(nc.scalar.copy, c_banks[0], c_grp[:], 0)
+        evacuate(nc.scalar.copy, w_banks[1], w_grp[:], 1)
+        evacuate(nc.scalar.copy, c_banks[1], c_grp[:], 1)
+
+        nc.vector.tensor_copy(
+            out=pm4[:].bitcast(F32).rearrange("p (c u) -> p c u", u=2),
+            in_=pw[:, 0:2].unsqueeze(1).to_broadcast([P, 2 * P, 2]),
+        )
+        scale_x(0, 0)
+        evacuate(nc.vector.tensor_copy, w_banks[0], w_grp[:], 0)
         code_tiles(0)
         quantise(state[("gx", 0)], *state[("xcodes", 0)])
-        scale_x(0, 0)
+        quantise_weights(w_grp, w_codes, w_scales, 0)
         scale_x(0, 1)
-        quantise(w_grp[:], w_codes[:], w_scales[:])
         nc.vector.tensor_copy(out=vec[:], in_=pv[:, 0:8])
         nc.vector.tensor_scalar_mul(out=cpm[:], in0=vec[:, 0:4], scalar1=SCALE)
         quantise(state[("gxs", 0)], *state[("ycodes", 0)])
-        quantise(c_grp[:], c_codes[:], c_scales[:])
+        quantise_weights(c_grp, c_codes, c_scales, 0)
+        quantise_weights(w_grp, w_codes, w_scales, 1)
+        quantise_weights(c_grp, c_codes, c_scales, 1)
 
         def unit(i):
             return 0 <= i < UNITS
@@ -280,10 +291,10 @@ def tile_neuroplasticitymodule_t_kernel(
             return [m for m in range(1, NM) if NJ * m - lead == step]
 
         for step in range(-7, UNITS + 4):
-            if unit(step + 3):
-                mx_z(step + 3)
             if unit(step + 1):
                 mx_g(step + 1)
+            if unit(step + 3):
+                mx_z(step + 3)
             if unit(step - 3):
                 out_transposes(step - 3)
             for h, lead in ((0, 11), (1, 9)):
@@ -293,13 +304,13 @@ def tile_neuroplasticitymodule_t_kernel(
                 add_pm(step - 2)
             if unit(step + 2):
                 sigmoid(step + 2)
+            if unit(step - 4):
+                out_copy(step - 4)
             for h, lead in ((0, 10), (1, 8)):
                 for m in prepared_at(step, lead):
                     in_copy(m, h)
-            if unit(step - 4):
-                out_copy(step - 4)
-            if unit(step + 0):
-                gate(step + 0)
+            if unit(step):
+                gate(step)
             if unit(step - 4):
                 finish(step - 4)
             for h, lead in ((0, 8), (1, 6)):

@@ -59,8 +59,10 @@ def tile_neuroplasticitymodule_t_kernel(
         out_view = out.rearrange("(m r i) j -> m r i j", r=P, i=4)
 
         nc.sync.dma_start(out=x_nat[0][:, firsts[0], :], in_=x_view[0][:, firsts[0], :])
+        pmw = const.tile([P, 4], BF16, name="pmw")
         nc.sync.dma_start(
-            out=vt[0:2, 128:384], in_=plasticity_modulation.rearrange("(u w) -> u w", u=2)
+            out=pmw[:].rearrange("p (u e) -> p u e", u=2),
+            in_=plasticity_modulation.rearrange("(u p e) -> p u e", u=2, e=2),
         )
         nc.sync.dma_start(out=x_nat[0][:, firsts[1], :], in_=x_view[0][:, firsts[1], :])
         nc.sync.dma_start(out=w_nat[:, firsts[0], :], in_=w_view[:, firsts[0], :])
@@ -101,10 +103,10 @@ def tile_neuroplasticitymodule_t_kernel(
             state[("xb", m, h)] = transpose_words(x_nat[m], h, "xin")
 
         def shared(i):
-            return i % NJ in SHARED and i < UNITS - NJ - 1
+            return i % NJ in SHARED and i < UNITS - NJ - 3
 
         def gp_affine(i):
-            return i % NJ in GP_AFFINE and i < UNITS - NJ - 1
+            return i % NJ in GP_AFFINE and i < UNITS - NJ + 1
 
         def in_copy(m, h):
             if h == 0:
@@ -227,12 +229,12 @@ def tile_neuroplasticitymodule_t_kernel(
                     out=o[:, :, cols], in0=state[("t", i)][:], in1=x_nat[m][:, :, cols],
                     op=ALU.mult,
                 )
-            if m < NM - 2:
+            if m < NM - 3:
                 pieces = [(0, H)] if jb == NJ - 1 else []
-            elif jb % 2 == 1:
-                pieces = [((jb - 1) * P, (jb + 1) * P)]
+            elif m < NM - 1:
+                pieces = [((jb - 1) * P, (jb + 1) * P)] if jb % 2 == 1 else []
             else:
-                pieces = []
+                pieces = [(jb * P, (jb + 1) * P)]
             for lo, hi in pieces:
                 nc.sync.dma_start(out=out_view[m][:, :, lo:hi], in_=o[:, :, lo:hi])
 
@@ -251,8 +253,6 @@ def tile_neuroplasticitymodule_t_kernel(
         cpm = const.tile([P, 4], F32, name="cpm")
 
         in_transposes(0, 0)
-        pw = ps.tile([P, P], F32, tag="t", name="pw")
-        nc.tensor.transpose(pw[:], vt[:, 128:384].bitcast(F32), ident_f[:])
         in_transposes(0, 1)
         w_banks = [transpose_words(w_nat, 0, "z")]
         pv = ps.tile([P, P], BF16, tag="t", name="pv")
@@ -263,16 +263,17 @@ def tile_neuroplasticitymodule_t_kernel(
 
         in_copy(0, 0)
         in_copy(0, 1)
+        evacuate(nc.scalar.copy, w_banks[0], w_grp[:], 0)
         evacuate(nc.scalar.copy, c_banks[0], c_grp[:], 0)
         evacuate(nc.scalar.copy, w_banks[1], w_grp[:], 1)
         evacuate(nc.scalar.copy, c_banks[1], c_grp[:], 1)
 
-        nc.vector.tensor_copy(
-            out=pm4[:].bitcast(F32).rearrange("p (c u) -> p c u", u=2),
-            in_=pw[:, 0:2].unsqueeze(1).to_broadcast([P, 2 * P, 2]),
+        nc.gpsimd.tensor_scalar(
+            out=pm4[:].rearrange("p (c t) -> p c t", t=4),
+            in0=pmw[:].unsqueeze(1).to_broadcast([P, 2 * P, 4]),
+            scalar1=1.0, scalar2=0.0, op0=ALU.mult, op1=ALU.add,
         )
         scale_x(0, 0)
-        evacuate(nc.vector.tensor_copy, w_banks[0], w_grp[:], 0)
         code_tiles(0)
         quantise(state[("gx", 0)], *state[("xcodes", 0)])
         quantise_weights(w_grp, w_codes, w_scales, 0)

@@ -71,9 +71,10 @@ def tile_neuroplasticitymodule_t_kernel(
         )
         nc.sync.dma_start(out=vt[4:8, 0:128], in_=b.rearrange("(a m) -> a m", a=4))
         nc.sync.dma_start(out=c_nat[:, firsts[0], :], in_=c_view[:, firsts[0], :])
+        nc.sync.dma_start(out=x_nat[1][:], in_=x_view[1])
         nc.sync.dma_start(out=w_nat[:, firsts[1], :], in_=w_view[:, firsts[1], :])
         nc.sync.dma_start(out=c_nat[:, firsts[1], :], in_=c_view[:, firsts[1], :])
-        for m in range(1, NM):
+        for m in range(2, NM):
             nc.sync.dma_start(out=x_nat[m][:], in_=x_view[m])
 
         def transpose_words(src, h, tag):
@@ -108,13 +109,13 @@ def tile_neuroplasticitymodule_t_kernel(
         def gp_affine(i):
             return i % NJ in GP_AFFINE and i < UNITS - NJ + 1
 
-        def in_copy(m, h):
+        def in_copy(m, h, copy=nc.scalar.copy):
             if h == 0:
                 both = grp.tile([P, 8 * ROWS], BF16, tag="gx", name="gx", align_bytes=64)
                 state[("both", m)] = both
                 state[("gx", m)] = both[:, 0 : 4 * ROWS]
                 state[("gxs", m)] = both[:, 4 * ROWS : 8 * ROWS]
-            evacuate(nc.scalar.copy, state[("xb", m, h)], state[("gx", m)], h)
+            evacuate(copy, state[("xb", m, h)], state[("gx", m)], h)
 
         def scale_x(m, h):
             half = state[("gxs", m)][:, h * 2 * ROWS : (h + 1) * 2 * ROWS]
@@ -201,7 +202,8 @@ def tile_neuroplasticitymodule_t_kernel(
             )
 
         def out_transposes(i):
-            t = ps.tile([P, 4, P], F32, tag="t", name="t")
+            spare = i >= UNITS - NJ and i % 2 == 1
+            t = ps.tile([P, 4, P], F32, tag="xin" if spare else "t", name="t")
             q = state[("q", i)]
             for rb in range(4):
                 nc.tensor.transpose(t[:, rb, :], q[:, rb * P : (rb + 1) * P], ident_f[:])
@@ -258,40 +260,45 @@ def tile_neuroplasticitymodule_t_kernel(
         pv = ps.tile([P, P], BF16, tag="t", name="pv")
         nc.tensor.transpose(pv[:], vt[:, 0:128], ident_b[:])
         c_banks = [transpose_words(c_nat, 0, "g")]
-        w_banks.append(transpose_words(w_nat, 1, "z"))
-        c_banks.append(transpose_words(c_nat, 1, "g"))
-
-        in_copy(0, 0)
+        in_copy(0, 0, nc.vector.tensor_copy)
         in_copy(0, 1)
         evacuate(nc.scalar.copy, w_banks[0], w_grp[:], 0)
         evacuate(nc.scalar.copy, c_banks[0], c_grp[:], 0)
-        evacuate(nc.scalar.copy, w_banks[1], w_grp[:], 1)
-        evacuate(nc.scalar.copy, c_banks[1], c_grp[:], 1)
-
         nc.gpsimd.tensor_scalar(
             out=pm4[:].rearrange("p (c t) -> p c t", t=4),
             in0=pmw[:].unsqueeze(1).to_broadcast([P, 2 * P, 4]),
             scalar1=1.0, scalar2=0.0, op0=ALU.mult, op1=ALU.add,
         )
         scale_x(0, 0)
+        in_transposes(1, 0)
         code_tiles(0)
+        nc.vector.tensor_copy(out=vec[:], in_=pv[:, 0:8])
+        scale_x(0, 1)
+        in_transposes(1, 1)
+        w_banks.append(transpose_words(w_nat, 1, "z"))
+        c_banks.append(transpose_words(c_nat, 1, "g"))
+        in_copy(1, 0)
+        in_copy(1, 1)
+        evacuate(nc.scalar.copy, w_banks[1], w_grp[:], 1)
+        evacuate(nc.scalar.copy, c_banks[1], c_grp[:], 1)
+        nc.vector.tensor_scalar_mul(out=cpm[:], in0=vec[:, 0:4], scalar1=SCALE)
         quantise(state[("gx", 0)], *state[("xcodes", 0)])
         quantise_weights(w_grp, w_codes, w_scales, 0)
-        scale_x(0, 1)
-        nc.vector.tensor_copy(out=vec[:], in_=pv[:, 0:8])
-        nc.vector.tensor_scalar_mul(out=cpm[:], in0=vec[:, 0:4], scalar1=SCALE)
         quantise(state[("gxs", 0)], *state[("ycodes", 0)])
         quantise_weights(c_grp, c_codes, c_scales, 0)
+        scale_x(1, 0)
+        scale_x(1, 1)
         quantise_weights(w_grp, w_codes, w_scales, 1)
+        quantise_both(1)
         quantise_weights(c_grp, c_codes, c_scales, 1)
 
         def unit(i):
             return 0 <= i < UNITS
 
         def prepared_at(step, lead):
-            return [m for m in range(1, NM) if NJ * m - lead == step]
+            return [m for m in range(2, NM) if NJ * m - lead == step]
 
-        for step in range(-7, UNITS + 4):
+        for step in range(-3, UNITS + 4):
             if unit(step + 1):
                 mx_g(step + 1)
             if unit(step + 3):
@@ -317,5 +324,5 @@ def tile_neuroplasticitymodule_t_kernel(
             for h, lead in ((0, 8), (1, 6)):
                 for m in prepared_at(step, lead):
                     scale_x(m, h)
-            if (step + 5) % NJ == 0 and 1 <= (step + 5) // NJ < NM:
+            if (step + 5) % NJ == 0 and 2 <= (step + 5) // NJ < NM:
                 quantise_both((step + 5) // NJ)

@@ -23,6 +23,8 @@ SCALE = 0.5 / H
 SHARED = (1, 3)
 GP_AFFINE = (1, 3)
 
+WARM_UP = 16
+
 FLOPS = 2 * 2 * B * H * H
 
 
@@ -39,6 +41,8 @@ def tile_neuroplasticitymodule_t_kernel(
         outp = ctx.enter_context(tc.tile_pool(name="outp", bufs=3))
         ps = ctx.enter_context(tc.psum_pool(name="ps", bufs=2))
 
+        zeros = const.tile([P, P], BF16, name="zeros")
+        nc.vector.memset(zeros[:], 0.0)
         vt = const.tile([P, 384], BF16, name="vt")
         nc.vector.memset(vt[:], 0.0)
         warm = const.tile([P, 2], F32, name="warm")
@@ -59,12 +63,12 @@ def tile_neuroplasticitymodule_t_kernel(
         out_view = out.rearrange("(m r i) j -> m r i j", r=P, i=4)
 
         nc.sync.dma_start(out=x_nat[0][:, firsts[0], :], in_=x_view[0][:, firsts[0], :])
+        nc.sync.dma_start(out=x_nat[0][:, firsts[1], :], in_=x_view[0][:, firsts[1], :])
         pmw = const.tile([P, 4], BF16, name="pmw")
         nc.sync.dma_start(
             out=pmw[:].rearrange("p (u e) -> p u e", u=2),
             in_=plasticity_modulation.rearrange("(u p e) -> p u e", u=2, e=2),
         )
-        nc.sync.dma_start(out=x_nat[0][:, firsts[1], :], in_=x_view[0][:, firsts[1], :])
         nc.sync.dma_start(out=w_nat[:, firsts[0], :], in_=w_view[:, firsts[0], :])
         nc.sync.dma_start(
             out=vt[0:4, 0:128], in_=plasticity_modulation.rearrange("(a m) -> a m", a=4)
@@ -117,13 +121,15 @@ def tile_neuroplasticitymodule_t_kernel(
                 state[("gxs", m)] = both[:, 4 * ROWS : 8 * ROWS]
             evacuate(copy, state[("xb", m, h)], state[("gx", m)], h)
 
+        pm_pairs = pmw[:].rearrange("p (u e) -> p u e", u=2)
+
         def scale_x(m, h):
             half = state[("gxs", m)][:, h * 2 * ROWS : (h + 1) * 2 * ROWS]
             words = state[("xb", m, h)][:].rearrange("p u c -> p (u c)").bitcast(BF16)
             nc.vector.tensor_tensor(
                 out=half.rearrange("p (c u e) -> p c u e", u=2, e=2),
                 in0=words.rearrange("p (u c e) -> p c u e", u=2, e=2),
-                in1=pm4[:].rearrange("p (c u e) -> p c u e", u=2, e=2),
+                in1=pm_pairs.unsqueeze(1).to_broadcast([P, 2 * P, 2, 2]),
                 op=ALU.mult,
             )
 
@@ -233,7 +239,7 @@ def tile_neuroplasticitymodule_t_kernel(
                 )
             if m < NM - 3:
                 pieces = [(0, H)] if jb == NJ - 1 else []
-            elif m < NM - 1:
+            elif i < UNITS - 6:
                 pieces = [((jb - 1) * P, (jb + 1) * P)] if jb % 2 == 1 else []
             else:
                 pieces = [(jb * P, (jb + 1) * P)]
@@ -246,7 +252,6 @@ def tile_neuroplasticitymodule_t_kernel(
 
         w_grp = const.tile([P, 4 * H], BF16, name="w_grp", align_bytes=64)
         c_grp = const.tile([P, 4 * H], BF16, name="c_grp", align_bytes=64)
-        pm4 = const.tile([P, 2 * ROWS], BF16, name="pm4", align_bytes=64)
         w_codes = const.tile([P, H], U32, name="w_codes", align_bytes=64)
         w_scales = const.tile([P, H], U8, name="w_scales", align_bytes=64)
         c_codes = const.tile([P, H], U32, name="c_codes", align_bytes=64)
@@ -254,6 +259,9 @@ def tile_neuroplasticitymodule_t_kernel(
         vec = const.tile([P, 8], F32, name="vec")
         cpm = const.tile([P, 4], F32, name="cpm")
 
+        spin = ps.tile([P, P], F32, tag="g", name="spin")
+        for k in range(WARM_UP):
+            nc.tensor.matmul(spin[:], lhsT=zeros[:], rhs=zeros[:], start=True, stop=True)
         in_transposes(0, 0)
         in_transposes(0, 1)
         w_banks = [transpose_words(w_nat, 0, "z")]
@@ -264,11 +272,6 @@ def tile_neuroplasticitymodule_t_kernel(
         in_copy(0, 1)
         evacuate(nc.scalar.copy, w_banks[0], w_grp[:], 0)
         evacuate(nc.scalar.copy, c_banks[0], c_grp[:], 0)
-        nc.gpsimd.tensor_scalar(
-            out=pm4[:].rearrange("p (c t) -> p c t", t=4),
-            in0=pmw[:].unsqueeze(1).to_broadcast([P, 2 * P, 4]),
-            scalar1=1.0, scalar2=0.0, op0=ALU.mult, op1=ALU.add,
-        )
         scale_x(0, 0)
         in_transposes(1, 0)
         code_tiles(0)

@@ -239,10 +239,8 @@ def tile_neuroplasticitymodule_t_kernel(
                 )
             if m < NM - 3:
                 pieces = [(0, H)] if jb == NJ - 1 else []
-            elif i < UNITS - 6:
-                pieces = [((jb - 1) * P, (jb + 1) * P)] if jb % 2 == 1 else []
             else:
-                pieces = [(jb * P, (jb + 1) * P)]
+                pieces = [((jb - 1) * P, (jb + 1) * P)] if jb % 2 == 1 else []
             for lo, hi in pieces:
                 nc.sync.dma_start(out=out_view[m][:, :, lo:hi], in_=o[:, :, lo:hi])
 

from contextlib import ExitStack

import concourse.mybir as mybir
from concourse.masks import make_identity

F32 = mybir.dt.float32
BF16 = mybir.dt.bfloat16
U32 = mybir.dt.uint32
U8 = mybir.dt.uint8
FP8X4 = mybir.dt.float8_e4m3fn_x4
ALU = mybir.AluOpType
ACT = mybir.ActivationFunctionType

P = 128
B = 8192
H = 512
ROWS = 512
NM = B // ROWS
NJ = H // P
UNITS = NM * NJ
SCALE = 0.5 / H

SHARED = (1, 3)
GP_AFFINE = (1, 3)

WARM_UP = 16

FLOPS = 2 * 2 * B * H * H


def tile_neuroplasticitymodule_t_kernel(
    tc, x, W, b, plasticity_modulation, connectivity_mask, out
):
    nc = tc.nc
    with ExitStack() as ctx:
        ctx.enter_context(tc.manual_schedule())
        const = ctx.enter_context(tc.tile_pool(name="const", bufs=1))
        grp = ctx.enter_context(tc.tile_pool(name="grp", bufs=5))
        cod = ctx.enter_context(tc.tile_pool(name="cod", bufs=2))
        ew = ctx.enter_context(tc.tile_pool(name="ew", bufs=6))
        outp = ctx.enter_context(tc.tile_pool(name="outp", bufs=3))
        ps = ctx.enter_context(tc.psum_pool(name="ps", bufs=2))

        zeros = const.tile([P, P], BF16, name="zeros")
        nc.vector.memset(zeros[:], 0.0)
        vt = const.tile([P, 384], BF16, name="vt")
        nc.vector.memset(vt[:], 0.0)
        warm = const.tile([P, 2], F32, name="warm")
        nc.vector.memset(warm[:], 0.0)
        nc.scalar.activation(out=warm[:, 1:2], in_=warm[:, 0:1], func=ACT.Sigmoid)
        ident_f = const.tile([P, P], F32, name="ident_f")
        make_identity(nc, ident_f[:])
        ident_b = const.tile([P, P], BF16, name="ident_b")
        make_identity(nc, ident_b[:])

        w_nat = const.tile([P, NJ, H], BF16, name="w_nat")
        c_nat = const.tile([P, NJ, H], BF16, name="c_nat")
        x_nat = [const.tile([P, 4, H], BF16, name="x_nat%d" % m) for m in range(NM)]
        x_view = x.rearrange("(m r i) k -> m r i k", r=P, i=4)
        w_view = W.rearrange("(a p) k -> p a k", p=P)
        c_view = connectivity_mask.rearrange("(a p) k -> p a k", p=P)
        firsts = [slice(0, 2), slice(2, 4)]
        out_view = out.rearrange("(m r i) j -> m r i j", r=P, i=4)

        nc.sync.dma_start(out=x_nat[0][:, firsts[0], :], in_=x_view[0][:, firsts[0], :])
        nc.sync.dma_start(out=x_nat[0][:, firsts[1], :], in_=x_view[0][:, firsts[1], :])
        pmw = const.tile([P, 4], BF16, name="pmw")
        nc.sync.dma_start(
            out=pmw[:].rearrange("p (u e) -> p u e", u=2),
            in_=plasticity_modulation.rearrange("(u p e) -> p u e", u=2, e=2),
        )
        nc.sync.dma_start(out=w_nat[:, firsts[0], :], in_=w_view[:, firsts[0], :])
        nc.sync.dma_start(
            out=vt[0:4, 0:128], in_=plasticity_modulation.rearrange("(a m) -> a m", a=4)
        )
        nc.sync.dma_start(out=vt[4:8, 0:128], in_=b.rearrange("(a m) -> a m", a=4))
        nc.sync.dma_start(out=c_nat[:, firsts[0], :], in_=c_view[:, firsts[0], :])
        nc.sync.dma_start(out=x_nat[1][:], in_=x_view[1])
        nc.sync.dma_start(out=w_nat[:, firsts[1], :], in_=w_view[:, firsts[1], :])
        nc.sync.dma_start(out=c_nat[:, firsts[1], :], in_=c_view[:, firsts[1], :])
        for m in range(2, NM):
            nc.sync.dma_start(out=x_nat[m][:], in_=x_view[m])

        def transpose_words(src, h, tag):
            bank = ps.tile([P, 2, 256], F32, tag=tag, name="bank_" + tag)
            for rr in range(2):
                words = src[:, 2 * h + rr, :].bitcast(F32)
                for u in range(2):
                    nc.tensor.transpose(
                        bank[:, u, rr * P : (rr + 1) * P],
                        words[:, u * P : (u + 1) * P],
                        ident_f[:],
                    )
            return bank

        def evacuate(copy, bank, grouped, h):
            dst = grouped.bitcast(F32).rearrange("p (c u) -> p c u", u=2)
            copy(out=dst[:, h * 256 : (h + 1) * 256, :], in_=bank[:].rearrange("p u c -> p c u"))

        def quantise(grouped, codes, scales):
            nc.vector.quantize_mx(
                out=codes.bitcast(FP8X4), scales=scales, in_=grouped
            )

        state = {}

        def in_transposes(m, h):
            state[("xb", m, h)] = transpose_words(x_nat[m], h, "xin")

        def shared(i):
            return i % NJ in SHARED and i < UNITS - NJ - 3

        def gp_affine(i):
            return i % NJ in GP_AFFINE and i < UNITS - NJ + 1

        def in_copy(m, h, copy=nc.scalar.copy):
            if h == 0:
                both = grp.tile([P, 8 * ROWS], BF16, tag="gx", name="gx", align_bytes=64)
                state[("both", m)] = both
                state[("gx", m)] = both[:, 0 : 4 * ROWS]
                state[("gxs", m)] = both[:, 4 * ROWS : 8 * ROWS]
            evacuate(copy, state[("xb", m, h)], state[("gx", m)], h)

        pm_pairs = pmw[:].rearrange("p (u e) -> p u e", u=2)

        def scale_x(m, h):
            half = state[("gxs", m)][:, h * 2 * ROWS : (h + 1) * 2 * ROWS]
            words = state[("xb", m, h)][:].rearrange("p u c -> p (u c)").bitcast(BF16)
            nc.vector.tensor_tensor(
                out=half.rearrange("p (c u e) -> p c u e", u=2, e=2),
                in0=words.rearrange("p (u c e) -> p c u e", u=2, e=2),
                in1=pm_pairs.unsqueeze(1).to_broadcast([P, 2 * P, 2, 2]),
                op=ALU.mult,
            )

        def code_tiles(m):
            codes = cod.tile([P, 2 * ROWS], U32, tag="xc", name="xc", align_bytes=64)
            scales = cod.tile([P, 2 * ROWS], U8, tag="xs", name="xs", align_bytes=64)
            state[("xcodes", m)] = (codes[:, 0:ROWS], scales[:, 0:ROWS])
            state[("ycodes", m)] = (codes[:, ROWS : 2 * ROWS], scales[:, ROWS : 2 * ROWS])
            return codes, scales

        def quantise_both(m):
            codes, scales = code_tiles(m)
            quantise(state[("both", m)][:], codes[:], scales[:])

        def mx_z(i):
            m, jb = divmod(i, NJ)
            cols = slice(jb * P, (jb + 1) * P)
            xc, xs = state[("xcodes", m)]
            z = ps.tile([P, ROWS], F32, tag="z", name="z")
            nc.tensor.matmul_mx(
                out=z[:],
                lhsT=w_codes[:, cols].bitcast(FP8X4),
                lhsT_scale=w_scales[:, cols],
                rhs=xc.bitcast(FP8X4),
                rhs_scale=xs,
                start=True,
                stop=True,
            )
            state[("z", i)] = z

        def mx_g(i):
            m, jb = divmod(i, NJ)
            cols = slice(jb * P, (jb + 1) * P)
            yc, ys = state[("ycodes", m)]
            g = ps.tile([P, ROWS], F32, tag="g", name="g")
            nc.tensor.matmul_mx(
                out=g[:],
                lhsT=c_codes[:, cols].bitcast(FP8X4),
                lhsT_scale=c_scales[:, cols],
                rhs=yc.bitcast(FP8X4),
                rhs_scale=ys,
                start=True,
                stop=True,
            )
            state[("g", i)] = g

        def sigmoid(i):
            jb = i % NJ
            s = ew.tile([P, ROWS], F32, tag="s", name="s")
            nc.scalar.activation(
                out=s[:], in_=state[("z", i)][:], func=ACT.Sigmoid,
                bias=vec[:, 4 + jb : 5 + jb], scale=1.0,
            )
            state[("s", i)] = s

        def gate(i):
            u = ew.tile([P, ROWS], F32, tag="u", name="u")
            nc.vector.tensor_tensor(
                out=u[:], in0=state[("g", i)][:], in1=state[("s", i)][:], op=ALU.mult
            )
            state[("u", i)] = u

        def add_pm(i):
            jb = i % NJ
            q = ew.tile([P, ROWS], F32, tag="q", name="q")
            state[("q", i)] = q
            if gp_affine(i):
                nc.gpsimd.tensor_scalar(
                    out=q[:], in0=state[("u", i)][:], scalar1=cpm[:, jb : jb + 1],
                    scalar2=vec[:, jb : jb + 1], op0=ALU.mult, op1=ALU.add,
                )
                return
            nc.scalar.activation(
                out=q[:], in_=state[("u", i)][:], func=ACT.Identity,
                bias=vec[:, jb : jb + 1], scale=cpm[:, jb : jb + 1],
            )

        def out_transposes(i):
            spare = i >= UNITS - NJ and i % 2 == 1
            t = ps.tile([P, 4, P], F32, tag="xin" if spare else "t", name="t")
            q = state[("q", i)]
            for rb in range(4):
                nc.tensor.transpose(t[:, rb, :], q[:, rb * P : (rb + 1) * P], ident_f[:])
            state[("t", i)] = t

        def out_copy(i):
            if shared(i):
                tcopy = ew.tile([P, 4, P], F32, tag="tc", name="tcopy")
                nc.scalar.copy(out=tcopy[:], in_=state[("t", i)][:])
                state[("tc", i)] = tcopy

        def finish(i):
            m, jb = divmod(i, NJ)
            cols = slice(jb * P, (jb + 1) * P)
            if jb == 0:
                state[("o", m)] = outp.tile([P, 4, H], F32, tag="o", name="o")
            o = state[("o", m)]
            if shared(i):
                nc.gpsimd.tensor_tensor(
                    out=o[:, :, cols], in0=state[("tc", i)][:], in1=x_nat[m][:, :, cols],
                    op=ALU.mult,
                )
            else:
                nc.vector.tensor_tensor(
                    out=o[:, :, cols], in0=state[("t", i)][:], in1=x_nat[m][:, :, cols],
                    op=ALU.mult,
                )
            if m < NM - 3:
                pieces = [(0, H)] if jb == NJ - 1 else []
            else:
                pieces = [((jb - 1) * P, (jb + 1) * P)] if jb % 2 == 1 else []
            for lo, hi in pieces:
                nc.sync.dma_start(out=out_view[m][:, :, lo:hi], in_=o[:, :, lo:hi])

        def quantise_weights(grouped, codes, scales, h):
            cols = slice(h * 256, (h + 1) * 256)
            quantise(grouped[:, h * 2 * H : (h + 1) * 2 * H], codes[:, cols], scales[:, cols])

        w_grp = const.tile([P, 4 * H], BF16, name="w_grp", align_bytes=64)
        c_grp = const.tile([P, 4 * H], BF16, name="c_grp", align_bytes=64)
        w_codes = const.tile([P, H], U32, name="w_codes", align_bytes=64)
        w_scales = const.tile([P, H], U8, name="w_scales", align_bytes=64)
        c_codes = const.tile([P, H], U32, name="c_codes", align_bytes=64)
        c_scales = const.tile([P, H], U8, name="c_scales", align_bytes=64)
        vec = const.tile([P, 8], F32, name="vec")
        cpm = const.tile([P, 4], F32, name="cpm")

        spin = ps.tile([P, P], F32, tag="g", name="spin")
        for k in range(WARM_UP):
            nc.tensor.matmul(spin[:], lhsT=zeros[:], rhs=zeros[:], start=True, stop=True)
        in_transposes(0, 0)
        in_transposes(0, 1)
        w_banks = [transpose_words(w_nat, 0, "z")]
        pv = ps.tile([P, P], BF16, tag="t", name="pv")
        nc.tensor.transpose(pv[:], vt[:, 0:128], ident_b[:])
        c_banks = [transpose_words(c_nat, 0, "g")]
        in_copy(0, 0, nc.vector.tensor_copy)
        in_copy(0, 1)
        evacuate(nc.scalar.copy, w_banks[0], w_grp[:], 0)
        evacuate(nc.scalar.copy, c_banks[0], c_grp[:], 0)
        scale_x(0, 0)
        in_transposes(1, 0)
        code_tiles(0)
        nc.vector.tensor_copy(out=vec[:], in_=pv[:, 0:8])
        scale_x(0, 1)
        in_transposes(1, 1)
        w_banks.append(transpose_words(w_nat, 1, "z"))
        c_banks.append(transpose_words(c_nat, 1, "g"))
        in_copy(1, 0)
        in_copy(1, 1)
        evacuate(nc.scalar.copy, w_banks[1], w_grp[:], 1)
        evacuate(nc.scalar.copy, c_banks[1], c_grp[:], 1)
        nc.vector.tensor_scalar_mul(out=cpm[:], in0=vec[:, 0:4], scalar1=SCALE)
        quantise(state[("gx", 0)], *state[("xcodes", 0)])
        quantise_weights(w_grp, w_codes, w_scales, 0)
        quantise(state[("gxs", 0)], *state[("ycodes", 0)])
        quantise_weights(c_grp, c_codes, c_scales, 0)
        scale_x(1, 0)
        scale_x(1, 1)
        quantise_weights(w_grp, w_codes, w_scales, 1)
        quantise_both(1)
        quantise_weights(c_grp, c_codes, c_scales, 1)

        def unit(i):
            return 0 <= i < UNITS

        def prepared_at(step, lead):
            return [m for m in range(2, NM) if NJ * m - lead == step]

        for step in range(-3, UNITS + 4):
            if unit(step + 1):
                mx_g(step + 1)
            if unit(step + 3):
                mx_z(step + 3)
            if unit(step - 3):
                out_transposes(step - 3)
            for h, lead in ((0, 11), (1, 9)):
                for m in prepared_at(step, lead):
                    in_transposes(m, h)
            if unit(step - 2):
                add_pm(step - 2)
            if unit(step + 2):
                sigmoid(step + 2)
            if unit(step - 4):
                out_copy(step - 4)
            for h, lead in ((0, 10), (1, 8)):
                for m in prepared_at(step, lead):
                    in_copy(m, h)
            if unit(step):
                gate(step)
            if unit(step - 4):
                finish(step - 4)
            for h, lead in ((0, 8), (1, 6)):
                for m in prepared_at(step, lead):
                    scale_x(m, h)
            if (step + 5) % NJ == 0 and 2 <= (step + 5) // NJ < NM:
                quantise_both((step + 5) // NJ)
